import numpy as np
import ml_dtypes


def mxq(x, axis, fmt="e4m3"):
    dtype, down = {"e4m3": (ml_dtypes.float8_e4m3fn, 7), "e5m2": (ml_dtypes.float8_e5m2, 14)}[fmt]
    v = np.moveaxis(np.asarray(x, np.float32).astype(ml_dtypes.bfloat16).astype(np.float64), axis, -1)
    blocks = v.reshape(v.shape[:-1] + (-1, 32))
    amax = np.abs(blocks).max(-1, keepdims=True)
    byte = np.maximum(np.where(amax > 0, np.frexp(amax)[1] - 1 + 127, 0) - down, 1)
    scale = np.exp2(byte - 127.0)
    codes = (blocks / scale).astype(np.float32).astype(dtype).astype(np.float64)
    return np.moveaxis((codes * scale).reshape(v.shape), -1, axis)


WIDE = False


def mx_kscale(k):
    if not WIDE:
        return np.ones(k)
    levels = np.array([10, -10, 5, -5, 0])
    if k % 512:
        return np.exp2(np.random.permutation(np.resize(levels, k // 32))).repeat(32)
    a = np.empty((k // 512, 16))
    for p in range(k // 512):
        a[p, :8] = np.random.permutation(np.resize(levels, 8))
        for g in range(8):
            far = levels[np.abs(levels - a[p, g]) >= 10]
            a[p, g + 8] = far[np.random.randint(len(far))]
    return np.exp2(a.ravel()).repeat(32)


BF16 = ml_dtypes.bfloat16


def bf(x):
    return np.asarray(x, np.float32).astype(BF16)


def f64(x):
    return np.asarray(x).astype(np.float64)


B, GH, GW, F_IN, F_OUT = 2, 128, 64, 512, 128


def setup_inputs():
    s = mx_kscale(F_IN)
    return {"X": bf(np.random.standard_normal((B, GH * GW, F_IN)) * s),
            "W_gcn": bf(np.random.standard_normal((F_IN, F_OUT)) * 0.5 / np.sqrt(F_IN) / s[:, None]),
            "b": bf(np.random.standard_normal(F_OUT) * 0.3),
            "H": GH, "Wd": GW}


def _neighbor_sum(Xg):
    p = np.pad(Xg, ((0, 0), (1, 1), (1, 1), (0, 0)))
    return (p[:, :-2, 1:-1] + p[:, 2:, 1:-1]
            + p[:, 1:-1, :-2] + p[:, 1:-1, 2:])


def reference(X, W_gcn, b, H, Wd):
    X = f64(X)
    Bn, N, F = X.shape
    Xg = X.reshape(Bn, H, Wd, F)
    AX = _neighbor_sum(Xg).reshape(Bn, N, F)
    return (mxq(AX, 2, "e4m3") @ mxq(f64(W_gcn), 0, "e4m3")) + f64(b)

@@ -1,0 +1,304 @@
+from contextlib import ExitStack
+
+import concourse.mybir as mybir
+from concourse.masks import make_identity
+
+F32 = mybir.dt.float32
+BF16 = mybir.dt.bfloat16
+U32 = mybir.dt.uint32
+U8 = mybir.dt.uint8
+FP8X4 = mybir.dt.float8_e4m3fn_x4
+ADD = mybir.AluOpType.add
+
+P = 128
+NB, GH, GW, F_IN, F_OUT = 2, 128, 64, 512, 128
+FLOPS = 2 * NB * GH * GW * F_IN * F_OUT
+
+JC = 8
+NCH = GW // JC
+NS = 24
+XI = 132
+XS = XI * 4
+DS = 520
+G_J = 4
+
+
+def pieces(starts, n):
+    cuts = [0, n]
+    for st in starts:
+        k = NS - st % NS
+        while k < n:
+            cuts.append(k)
+            k += NS
+    cs = sorted(set(cuts))
+    return [(cs[i], cs[i + 1] - cs[i]) for i in range(len(cs) - 1)]
+
+
+def stream(bb, j):
+    return 1 + bb * (GW + 1) + j
+
+
+def tile_graphconvlayer_t_kernel(tc, X, W_gcn, b, H, Wd, out):
+    nc = tc.nc
+    assert H == GH and Wd == GW
+    xv = X.rearrange("b (i j) f -> b i (j f)", j=GW)
+    outv = out.rearrange("b (i j) o -> b i (j o)", j=GW)
+
+    with ExitStack() as ctx:
+        const = ctx.enter_context(tc.tile_pool(name="const", bufs=1))
+        xpool = ctx.enter_context(tc.tile_pool(name="xin", bufs=4))
+        ggpool = ctx.enter_context(tc.tile_pool(name="grouped_g", bufs=1))
+        gvpool = ctx.enter_context(tc.tile_pool(name="grouped_v", bufs=2))
+        qpool = ctx.enter_context(tc.tile_pool(name="quant", bufs=2))
+        opool = ctx.enter_context(tc.tile_pool(name="outsb", bufs=3))
+        pst = ctx.enter_context(tc.psum_pool(name="pst", bufs=4))
+        psy = ctx.enter_context(tc.psum_pool(name="psy", bufs=2))
+        pso = ctx.enter_context(tc.psum_pool(name="pso", bufs=2))
+        ypool = ctx.enter_context(tc.tile_pool(name="ysb", bufs=3))
+
+        ctx.enter_context(tc.manual_schedule())
+
+        ident = const.tile([P, P], F32)
+        make_identity(nc, ident[:])
+
+        xtw = const.tile([P, NS * XI * 2], F32)
+        xtw4 = xtw[:].rearrange("p (s i u) -> p s i u", i=XI, u=2)
+        nc.vector.memset(xtw4[:, :, GH : GH + 4, :], 0.0)
+        xtb = xtw[:].bitcast(BF16).rearrange("p (s c) -> p s c", c=XS)
+        dr = const.tile([P, NS * DS], F32)
+        dv = dr[:].rearrange("p (s c) -> p s c", c=DS)
+
+        wraw = const.tile([P, 2, 2 * F_OUT], BF16)
+        nc.scalar.dma_start(out=wraw[:], in_=W_gcn.rearrange("(p u e) c -> p u (e c)", u=2, e=2))
+        braw = const.tile([P, F_OUT], BF16)
+        nc.scalar.dma_start(out=braw[:], in_=b.partition_broadcast(P))
+        wg = const.tile([P, 4 * F_OUT], BF16, align_bytes=64)
+        wc = const.tile([P, F_OUT], U32, align_bytes=64)
+        ws = const.tile([P, F_OUT], U8, align_bytes=64)
+        bdiag = const.tile([P, F_OUT], F32)
+        bcol = const.tile([P, 1], F32)
+        bias4 = const.tile([P, 4, F_OUT], F32)
+
+        def emit_constants():
+            nc.vector.tensor_copy(
+                out=wg[:].rearrange("p (c u e) -> p c u e", u=2, e=2),
+                in_=wraw[:].rearrange("p u (e c) -> p c u e", e=2),
+            )
+            nc.vector.tensor_tensor(out=bdiag[:], in0=braw[:], in1=ident[:], op=mybir.AluOpType.mult)
+            nc.vector.quantize_mx(out=wc[:].bitcast(FP8X4), scales=ws[:], in_=wg[:])
+            nc.vector.tensor_reduce(out=bcol[:], in_=bdiag[:], axis=mybir.AxisListType.X, op=ADD)
+            for a in range(4):
+                nc.vector.tensor_copy(out=bias4[:, a, :], in_=braw[:])
+
+        n_chunks = NB * NCH
+        xin_of = {}
+        bank_of = {}
+        gg_of = {}
+        gv_of = {}
+        q_of = {}
+        y_of = {}
+        o_of = {}
+
+        def emit_load(k):
+            bb, c = k // NCH, k % NCH
+            xin = xpool.tile([P, JC * F_IN], BF16)
+            n_dma = 4 if k == 0 else 1
+            w = JC * F_IN // n_dma
+            for d in range(n_dma):
+                lo = c * JC * F_IN + d * w
+                nc.sync.dma_start(out=xin[:, d * w : (d + 1) * w], in_=xv[bb, :, lo : lo + w])
+            xin_of[k] = xin
+
+        def emit_front(m):
+            bb, c, pair = m // (4 * NCH), (m // 4) % NCH, m % 4
+            xw = xin_of[m // 4][:].bitcast(F32)
+            bank = pst.tile([P, 4, P], F32)
+            for q in range(4):
+                u, jl = q // 2, q % 2
+                col = (pair * 2 + jl) * 2 * P
+                nc.tensor.transpose(out=bank[:, q, :], in_=xw[:, col + u : col + 2 * P : 2], identity=ident[:])
+            s0 = stream(bb, c * JC + 2 * pair)
+            for off, n in pieces([s0], 2):
+                r = (s0 + off) % NS
+                nc.scalar.copy(
+                    out=xtw4[:, r : r + n, 1 : 1 + GH, :],
+                    in_=bank[:].rearrange("p (u j) i -> p j i u", u=2)[:, off : off + n],
+                )
+            bank_of[m] = bank
+
+        def emit_edges(k):
+            bb, c = k // NCH, k % NCH
+            s0 = stream(bb, c * JC)
+            if c == 0:
+                r = (s0 - 1) % NS
+                nc.vector.tensor_copy(out=dv[:, r : r + 1, 4:520], in_=xtb[:, s0 % NS : s0 % NS + 1, 4:520])
+            if c == NCH - 1:
+                z = (s0 + JC) % NS
+                nc.vector.memset(xtw4[:, z : z + 1, :, :], 0.0)
+
+        def emit_fill(m):
+            bb, c, pair = m // (4 * NCH), (m // 4) % NCH, m % 4
+            s0 = stream(bb, c * JC + 2 * pair)
+            for off, n in pieces([s0, s0 + 1], 2):
+                r = (s0 + off) % NS
+                r1 = (s0 + off + 1) % NS
+                nc.scalar.copy(out=dv[:, r : r + n, 4:8], in_=xtb[:, r1 : r1 + n, 4:8])
+
+        def emit_pairsums(m):
+            bb, c, pair = m // (4 * NCH), (m // 4) % NCH, m % 4
+            s0 = stream(bb, c * JC + 2 * pair)
+            bankb = bank_of[m][:].rearrange("p q i -> p (q i)").bitcast(BF16)
+            bankv = bankb.rearrange("p (u j i e) -> p j i u e", u=2, j=2, e=2)
+            for off, n in pieces([s0, s0 + 1], 2):
+                r = (s0 + off) % NS
+                r1 = (s0 + off + 1) % NS
+                nc.vector.tensor_tensor(
+                    out=dv[:, r : r + n, 8:520].rearrange("p j (i u e) -> p j i u e", u=2, e=2),
+                    in0=bankv[:, off : off + n],
+                    in1=xtb[:, r1 : r1 + n, 8:520].rearrange("p j (i u e) -> p j i u e", u=2, e=2),
+                    op=ADD,
+                )
+
+        def second_add(eng, g, k, lo, cnt):
+            s0 = stream(k // NCH, (k % NCH) * JC)
+            for off, n in pieces([s0 + lo, s0 + lo - 1], cnt):
+                r = (s0 + lo + off) % NS
+                rm = (s0 + lo + off - 1) % NS
+                eng.tensor_tensor(
+                    out=g[:, (lo + off) % 4 : (lo + off) % 4 + n, :],
+                    in0=dv[:, r : r + n, 4:516],
+                    in1=dv[:, rm : rm + n, 8:520],
+                    op=ADD,
+                )
+
+        def emit_low_half(k, eng, cnt):
+            gg = ggpool.tile([P, 4, F_IN], BF16, align_bytes=64)
+            gg_of[k] = gg
+            if k == 0:
+                nc.vector.memset(gg[:, 0, 0:16], 0.0)
+            second_add(eng, gg, k, 0, cnt)
+
+        def emit_high_half(k):
+            gv = gvpool.tile([P, 4, F_IN], BF16, align_bytes=64)
+            gv_of[k] = gv
+            second_add(nc.vector, gv, k, 4, 4)
+
+        def emit_quant(k, h):
+            if k not in q_of:
+                codes = qpool.tile([P, JC * P], U32, align_bytes=64)
+                scl = qpool.tile([P, JC * P], U8, align_bytes=64)
+                q_of[k] = (codes, scl)
+            codes, scl = q_of[k]
+            g = gg_of[k] if h == 0 else gv_of[k]
+            cols = slice(h * 4 * P, (h + 1) * 4 * P)
+            nc.vector.quantize_mx(
+                out=codes[:, cols].bitcast(FP8X4), scales=scl[:, cols], in_=g[:].rearrange("p j c -> p (j c)")
+            )
+
+        def emit_product(k, h):
+            codes, scl = q_of[k]
+            cols = slice(h * 4 * P, (h + 1) * 4 * P)
+            py = psy.tile([P, 4 * P], F32)
+            nc.tensor.matmul_mx(
+                out=py[:],
+                lhsT=wc[:].bitcast(FP8X4),
+                lhsT_scale=ws[:],
+                rhs=codes[:, cols].bitcast(FP8X4),
+                rhs_scale=scl[:, cols],
+                start=True,
+                stop=True,
+            )
+            ysb = ypool.tile([P, 4 * P], F32)
+            nc.scalar.activation(
+                out=ysb[:], in_=py[:], func=mybir.ActivationFunctionType.Identity, bias=bcol[:, 0:1], scale=1.0
+            )
+            y_of[(k, h)] = ysb
+
+        def out_tile(k):
+            if k not in o_of:
+                osb = opool.tile([P, JC, F_OUT], F32)
+                o_of[k] = osb
+            return o_of[k]
+
+        def emit_turn_back(k, h):
+            ysb = y_of[(k, h)]
+            po = pso.tile([P, 4, F_OUT], F32)
+            for a in range(4):
+                nc.tensor.transpose(out=po[:, a, :], in_=ysb[:, a * P : (a + 1) * P], identity=ident[:])
+            nc.scalar.copy(out=out_tile(k)[:, h * 4 : (h + 1) * 4, :], in_=po[:])
+
+        def emit_direct(k, h):
+            codes, scl = q_of[k]
+            po = pso.tile([P, 4, F_OUT], F32)
+            for a in range(4):
+                jl = h * 4 + a
+                nc.tensor.matmul_mx(
+                    out=po[:, a, :],
+                    lhsT=codes[:, jl * P : (jl + 1) * P].bitcast(FP8X4),
+                    lhsT_scale=scl[:, jl * P : (jl + 1) * P],
+                    rhs=wc[:].bitcast(FP8X4),
+                    rhs_scale=ws[:],
+                    start=True,
+                    stop=True,
+                )
+            nc.vector.tensor_tensor(out=out_tile(k)[:, h * 4 : (h + 1) * 4, :], in0=po[:], in1=bias4[:], op=ADD)
+
+        def emit_store(k, lo, cnt):
+            bb, c = k // NCH, k % NCH
+            a = (c * JC + lo) * F_OUT
+            nc.sync.dma_start(
+                out=outv[bb, :, a : a + cnt * F_OUT],
+                in_=out_tile(k)[:, lo : lo + cnt, :].rearrange("p j o -> p (j o)"),
+            )
+
+        for k in range(3):
+            emit_load(k)
+        emit_constants()
+        for m in range(4):
+            emit_front(m)
+        emit_edges(0)
+        for m in range(3):
+            emit_fill(m)
+        last = n_chunks - 1
+        for k in range(n_chunks):
+            emit_pairsums(4 * k)
+            if k >= 2:
+                emit_product(k - 2, 0)
+                emit_product(k - 2, 1)
+            if k < last:
+                emit_front(4 * (k + 1))
+            emit_fill(4 * k + 3)
+            emit_pairsums(4 * k + 1)
+            if k >= 2:
+                emit_turn_back(k - 2, 0)
+                emit_turn_back(k - 2, 1)
+                emit_store(k - 2, 0, JC)
+            emit_pairsums(4 * k + 2)
+            emit_pairsums(4 * k + 3)
+            emit_high_half(k)
+            if k < last:
+                emit_edges(k + 1)
+            if k >= 1:
+                emit_quant(k - 1, 1)
+                emit_quant(k - 1, 0)
+            if k < last:
+                emit_low_half(k, nc.gpsimd, G_J)
+                for pair in range(1, 4):
+                    emit_front(4 * (k + 1) + pair)
+                for pair in range(3):
+                    emit_fill(4 * (k + 1) + pair)
+            if k + 3 < n_chunks:
+                emit_load(k + 3)
+        emit_quant(last, 1)
+        emit_low_half(last, nc.vector, 4)
+        emit_quant(last, 0)
+        for h in range(2):
+            emit_product(last - 1, h)
+        emit_product(last, 1)
+        for h in range(2):
+            emit_turn_back(last - 1, h)
+        emit_store(last - 1, 0, JC)
+        emit_turn_back(last, 1)
+        emit_store(last, 4, 4)
+        emit_direct(last, 0)
+        emit_store(last, 0, 4)

@@ -16,11 +16,10 @@ FLOPS = 2 * NB * GH * GW * F_IN * F_OUT
 
 JC = 8
 NCH = GW // JC
-NS = 24
+NS = 45
 XI = 132
 XS = XI * 4
 DS = 520
-G_J = 4
 
 
 def pieces(starts, n):
@@ -78,6 +77,9 @@ def tile_graphconvlayer_t_kernel(tc, X, W_gcn, b, H, Wd, out):
         bdiag = const.tile([P, F_OUT], F32)
         bcol = const.tile([P, 1], F32)
         bias4 = const.tile([P, 4, F_OUT], F32)
+        identb = const.tile([P, P], BF16)
+        adj = const.tile([P, P], BF16)
+        gp = const.tile([P, 4, F_IN], BF16, align_bytes=64)
 
         def emit_constants():
             nc.vector.tensor_copy(
@@ -89,6 +91,10 @@ def tile_graphconvlayer_t_kernel(tc, X, W_gcn, b, H, Wd, out):
             nc.vector.tensor_reduce(out=bcol[:], in_=bdiag[:], axis=mybir.AxisListType.X, op=ADD)
             for a in range(4):
                 nc.vector.tensor_copy(out=bias4[:, a, :], in_=braw[:])
+            nc.vector.tensor_copy(out=identb[:], in_=ident[:])
+            nc.vector.memset(adj[:, 0:2], 0.0)
+            nc.vector.tensor_copy(out=adj[:, 1:P], in_=ident[:, 0 : P - 1])
+            nc.vector.tensor_tensor(out=adj[:, 0 : P - 1], in0=adj[:, 0 : P - 1], in1=ident[:, 1:P], op=ADD)
 
         n_chunks = NB * NCH
         xin_of = {}
@@ -171,28 +177,41 @@ def tile_graphconvlayer_t_kernel(tc, X, W_gcn, b, H, Wd, out):
                     op=ADD,
                 )
 
-        def emit_low_half(k, eng, cnt):
+        def emit_low_half(k, cnt):
             gg = ggpool.tile([P, 4, F_IN], BF16, align_bytes=64)
             gg_of[k] = gg
             if k == 0:
                 nc.vector.memset(gg[:, 0, 0:16], 0.0)
-            second_add(eng, gg, k, 0, cnt)
+            second_add(nc.gpsimd, gg, k, 0, cnt)
+
+        def emit_plain(c):
+            xc = xin_of[last][:].rearrange("p (j f t) -> p j t f", j=JC, t=4)
+            po = pso.tile([P, 4, F_OUT], F32)
+            j = 4 + c
+            taps = [(j, adj), (j - 1, identb)] + ([(j + 1, identb)] if j + 1 < JC else [])
+            for t in range(4):
+                for n, (jj, moving) in enumerate(taps):
+                    nc.tensor.matmul(
+                        out=po[:, t, :], lhsT=xc[:, jj, t, :], rhs=moving[:], start=n == 0, stop=n == len(taps) - 1
+                    )
+            nc.scalar.copy(
+                out=gp[:, c, :].rearrange("p (i t) -> p i t", t=4), in_=po[:].rearrange("p t i -> p i t")
+            )
 
         def emit_high_half(k):
             gv = gvpool.tile([P, 4, F_IN], BF16, align_bytes=64)
             gv_of[k] = gv
             second_add(nc.vector, gv, k, 4, 4)
 
-        def emit_quant(k, h):
+        def emit_quant(k, h, g, lo=0, hi=4):
             if k not in q_of:
                 codes = qpool.tile([P, JC * P], U32, align_bytes=64)
                 scl = qpool.tile([P, JC * P], U8, align_bytes=64)
                 q_of[k] = (codes, scl)
             codes, scl = q_of[k]
-            g = gg_of[k] if h == 0 else gv_of[k]
-            cols = slice(h * 4 * P, (h + 1) * 4 * P)
+            cols = slice((h * 4 + lo) * P, (h * 4 + hi) * P)
             nc.vector.quantize_mx(
-                out=codes[:, cols].bitcast(FP8X4), scales=scl[:, cols], in_=g[:].rearrange("p j c -> p (j c)")
+                out=codes[:, cols].bitcast(FP8X4), scales=scl[:, cols], in_=g[:, lo:hi, :].rearrange("p j c -> p (j c)")
             )
 
         def emit_product(k, h):
@@ -227,11 +246,11 @@ def tile_graphconvlayer_t_kernel(tc, X, W_gcn, b, H, Wd, out):
                 nc.tensor.transpose(out=po[:, a, :], in_=ysb[:, a * P : (a + 1) * P], identity=ident[:])
             nc.scalar.copy(out=out_tile(k)[:, h * 4 : (h + 1) * 4, :], in_=po[:])
 
-        def emit_direct(k, h):
+        def emit_direct(k, lo, cnt):
             codes, scl = q_of[k]
             po = pso.tile([P, 4, F_OUT], F32)
-            for a in range(4):
-                jl = h * 4 + a
+            for a in range(cnt):
+                jl = lo + a
                 nc.tensor.matmul_mx(
                     out=po[:, a, :],
                     lhsT=codes[:, jl * P : (jl + 1) * P].bitcast(FP8X4),
@@ -241,7 +260,9 @@ def tile_graphconvlayer_t_kernel(tc, X, W_gcn, b, H, Wd, out):
                     start=True,
                     stop=True,
                 )
-            nc.vector.tensor_tensor(out=out_tile(k)[:, h * 4 : (h + 1) * 4, :], in0=po[:], in1=bias4[:], op=ADD)
+            nc.vector.tensor_tensor(
+                out=out_tile(k)[:, lo : lo + cnt, :], in0=po[:, 0:cnt, :], in1=bias4[:, 0:cnt, :], op=ADD
+            )
 
         def emit_store(k, lo, cnt):
             bb, c = k // NCH, k % NCH
@@ -260,45 +281,66 @@ def tile_graphconvlayer_t_kernel(tc, X, W_gcn, b, H, Wd, out):
         for m in range(3):
             emit_fill(m)
         last = n_chunks - 1
-        for k in range(n_chunks):
+        for k in range(last):
             emit_pairsums(4 * k)
             if k >= 2:
                 emit_product(k - 2, 0)
                 emit_product(k - 2, 1)
-            if k < last:
-                emit_front(4 * (k + 1))
+            emit_front(4 * (k + 1))
             emit_fill(4 * k + 3)
             emit_pairsums(4 * k + 1)
             if k >= 2:
                 emit_turn_back(k - 2, 0)
                 emit_turn_back(k - 2, 1)
                 emit_store(k - 2, 0, JC)
+            if k + 1 == last:
+                for c in range(2):
+                    emit_plain(c)
             emit_pairsums(4 * k + 2)
             emit_pairsums(4 * k + 3)
+            if k >= 1:
+                emit_quant(k - 1, 1, gv_of[k - 1])
             emit_high_half(k)
-            if k < last:
+            if k + 1 < last:
                 emit_edges(k + 1)
             if k >= 1:
-                emit_quant(k - 1, 1)
-                emit_quant(k - 1, 0)
-            if k < last:
-                emit_low_half(k, nc.gpsimd, G_J)
-                for pair in range(1, 4):
-                    emit_front(4 * (k + 1) + pair)
-                for pair in range(3):
-                    emit_fill(4 * (k + 1) + pair)
+                emit_quant(k - 1, 0, gg_of[k - 1])
+            emit_low_half(k, 4 if k + 1 < last else 2)
+            pairs = 4 if k + 1 < last else 3
+            for pair in range(1, pairs):
+                emit_front(4 * (k + 1) + pair)
+            for pair in range(pairs - 1):
+                emit_fill(4 * (k + 1) + pair)
             if k + 3 < n_chunks:
                 emit_load(k + 3)
-        emit_quant(last, 1)
-        emit_low_half(last, nc.vector, 4)
-        emit_quant(last, 0)
+
+        for c in range(2, 4):
+            emit_plain(c)
+
+        emit_pairsums(4 * last)
         for h in range(2):
-            emit_product(last - 1, h)
+            emit_product(last - 2, h)
+        emit_pairsums(4 * last + 1)
+        for h in range(2):
+            emit_turn_back(last - 2, h)
+        emit_store(last - 2, 0, JC)
+        emit_quant(last - 1, 1, gv_of[last - 1])
+        second_add(nc.vector, gg_of[last - 1], last - 1, 2, 2)
+        emit_quant(last, 1, gp)
+        emit_quant(last - 1, 0, gg_of[last - 1])
+        gv = gvpool.tile([P, 4, F_IN], BF16, align_bytes=64)
+        for lo in (0, 2):
+            second_add(nc.vector, gv, last, lo, 2)
+        for lo in (0, 2):
+            emit_quant(last, 0, gv, lo, lo + 2)
+        emit_product(last - 1, 1)
         emit_product(last, 1)
-        for h in range(2):
-            emit_turn_back(last - 1, h)
-        emit_store(last - 1, 0, JC)
+        emit_turn_back(last - 1, 1)
+        emit_store(last - 1, 4, 4)
         emit_turn_back(last, 1)
         emit_store(last, 4, 4)
-        emit_direct(last, 0)
-        emit_store(last, 0, 4)
+        emit_direct(last - 1, 0, 4)
+        emit_store(last - 1, 0, 4)
+        for lo in (0, 2):
+            emit_direct(last, lo, 2)
+            emit_store(last, lo, 2)

from contextlib import ExitStack

import concourse.mybir as mybir
from concourse.masks import make_identity

F32 = mybir.dt.float32
BF16 = mybir.dt.bfloat16
U32 = mybir.dt.uint32
U8 = mybir.dt.uint8
FP8X4 = mybir.dt.float8_e4m3fn_x4
ADD = mybir.AluOpType.add

P = 128
NB, GH, GW, F_IN, F_OUT = 2, 128, 64, 512, 128
FLOPS = 2 * NB * GH * GW * F_IN * F_OUT

JC = 8
NCH = GW // JC
NS = 45
XI = 132
XS = XI * 4
DS = 520


def pieces(starts, n):
    cuts = [0, n]
    for st in starts:
        k = NS - st % NS
        while k < n:
            cuts.append(k)
            k += NS
    cs = sorted(set(cuts))
    return [(cs[i], cs[i + 1] - cs[i]) for i in range(len(cs) - 1)]


def stream(bb, j):
    return 1 + bb * (GW + 1) + j


def tile_graphconvlayer_t_kernel(tc, X, W_gcn, b, H, Wd, out):
    nc = tc.nc
    assert H == GH and Wd == GW
    xv = X.rearrange("b (i j) f -> b i (j f)", j=GW)
    outv = out.rearrange("b (i j) o -> b i (j o)", j=GW)

    with ExitStack() as ctx:
        const = ctx.enter_context(tc.tile_pool(name="const", bufs=1))
        xpool = ctx.enter_context(tc.tile_pool(name="xin", bufs=4))
        ggpool = ctx.enter_context(tc.tile_pool(name="grouped_g", bufs=1))
        gvpool = ctx.enter_context(tc.tile_pool(name="grouped_v", bufs=2))
        qpool = ctx.enter_context(tc.tile_pool(name="quant", bufs=2))
        opool = ctx.enter_context(tc.tile_pool(name="outsb", bufs=3))
        pst = ctx.enter_context(tc.psum_pool(name="pst", bufs=4))
        psy = ctx.enter_context(tc.psum_pool(name="psy", bufs=2))
        pso = ctx.enter_context(tc.psum_pool(name="pso", bufs=2))
        ypool = ctx.enter_context(tc.tile_pool(name="ysb", bufs=3))

        ctx.enter_context(tc.manual_schedule())

        ident = const.tile([P, P], F32)
        make_identity(nc, ident[:])

        xtw = const.tile([P, NS * XI * 2], F32)
        xtw4 = xtw[:].rearrange("p (s i u) -> p s i u", i=XI, u=2)
        nc.vector.memset(xtw4[:, :, GH : GH + 4, :], 0.0)
        xtb = xtw[:].bitcast(BF16).rearrange("p (s c) -> p s c", c=XS)
        dr = const.tile([P, NS * DS], F32)
        dv = dr[:].rearrange("p (s c) -> p s c", c=DS)

        wraw = const.tile([P, 2, 2 * F_OUT], BF16)
        nc.scalar.dma_start(out=wraw[:], in_=W_gcn.rearrange("(p u e) c -> p u (e c)", u=2, e=2))
        braw = const.tile([P, F_OUT], BF16)
        nc.scalar.dma_start(out=braw[:], in_=b.partition_broadcast(P))
        wg = const.tile([P, 4 * F_OUT], BF16, align_bytes=64)
        wc = const.tile([P, F_OUT], U32, align_bytes=64)
        ws = const.tile([P, F_OUT], U8, align_bytes=64)
        bdiag = const.tile([P, F_OUT], F32)
        bcol = const.tile([P, 1], F32)
        bias4 = const.tile([P, 4, F_OUT], F32)
        identb = const.tile([P, P], BF16)
        adj = const.tile([P, P], BF16)
        gp = const.tile([P, 4, F_IN], BF16, align_bytes=64)

        def emit_constants():
            nc.vector.tensor_copy(
                out=wg[:].rearrange("p (c u e) -> p c u e", u=2, e=2),
                in_=wraw[:].rearrange("p u (e c) -> p c u e", e=2),
            )
            nc.vector.tensor_tensor(out=bdiag[:], in0=braw[:], in1=ident[:], op=mybir.AluOpType.mult)
            nc.vector.quantize_mx(out=wc[:].bitcast(FP8X4), scales=ws[:], in_=wg[:])
            nc.vector.tensor_reduce(out=bcol[:], in_=bdiag[:], axis=mybir.AxisListType.X, op=ADD)
            for a in range(4):
                nc.vector.tensor_copy(out=bias4[:, a, :], in_=braw[:])
            nc.vector.tensor_copy(out=identb[:], in_=ident[:])
            nc.vector.memset(adj[:, 0:2], 0.0)
            nc.vector.tensor_copy(out=adj[:, 1:P], in_=ident[:, 0 : P - 1])
            nc.vector.tensor_tensor(out=adj[:, 0 : P - 1], in0=adj[:, 0 : P - 1], in1=ident[:, 1:P], op=ADD)

        n_chunks = NB * NCH
        xin_of = {}
        bank_of = {}
        gg_of = {}
        gv_of = {}
        q_of = {}
        y_of = {}
        o_of = {}

        def emit_load(k):
            bb, c = k // NCH, k % NCH
            xin = xpool.tile([P, JC * F_IN], BF16)
            n_dma = 4 if k == 0 else 1
            w = JC * F_IN // n_dma
            for d in range(n_dma):
                lo = c * JC * F_IN + d * w
                nc.sync.dma_start(out=xin[:, d * w : (d + 1) * w], in_=xv[bb, :, lo : lo + w])
            xin_of[k] = xin

        def emit_front(m):
            bb, c, pair = m // (4 * NCH), (m // 4) % NCH, m % 4
            xw = xin_of[m // 4][:].bitcast(F32)
            bank = pst.tile([P, 4, P], F32)
            for q in range(4):
                u, jl = q // 2, q % 2
                col = (pair * 2 + jl) * 2 * P
                nc.tensor.transpose(out=bank[:, q, :], in_=xw[:, col + u : col + 2 * P : 2], identity=ident[:])
            s0 = stream(bb, c * JC + 2 * pair)
            for off, n in pieces([s0], 2):
                r = (s0 + off) % NS
                nc.scalar.copy(
                    out=xtw4[:, r : r + n, 1 : 1 + GH, :],
                    in_=bank[:].rearrange("p (u j) i -> p j i u", u=2)[:, off : off + n],
                )
            bank_of[m] = bank

        def emit_edges(k):
            bb, c = k // NCH, k % NCH
            s0 = stream(bb, c * JC)
            if c == 0:
                r = (s0 - 1) % NS
                nc.vector.tensor_copy(out=dv[:, r : r + 1, 4:520], in_=xtb[:, s0 % NS : s0 % NS + 1, 4:520])
            if c == NCH - 1:
                z = (s0 + JC) % NS
                nc.vector.memset(xtw4[:, z : z + 1, :, :], 0.0)

        def emit_fill(m):
            bb, c, pair = m // (4 * NCH), (m // 4) % NCH, m % 4
            s0 = stream(bb, c * JC + 2 * pair)
            for off, n in pieces([s0, s0 + 1], 2):
                r = (s0 + off) % NS
                r1 = (s0 + off + 1) % NS
                nc.scalar.copy(out=dv[:, r : r + n, 4:8], in_=xtb[:, r1 : r1 + n, 4:8])

        def emit_pairsums(m):
            bb, c, pair = m // (4 * NCH), (m // 4) % NCH, m % 4
            s0 = stream(bb, c * JC + 2 * pair)
            bankb = bank_of[m][:].rearrange("p q i -> p (q i)").bitcast(BF16)
            bankv = bankb.rearrange("p (u j i e) -> p j i u e", u=2, j=2, e=2)
            for off, n in pieces([s0, s0 + 1], 2):
                r = (s0 + off) % NS
                r1 = (s0 + off + 1) % NS
                nc.vector.tensor_tensor(
                    out=dv[:, r : r + n, 8:520].rearrange("p j (i u e) -> p j i u e", u=2, e=2),
                    in0=bankv[:, off : off + n],
                    in1=xtb[:, r1 : r1 + n, 8:520].rearrange("p j (i u e) -> p j i u e", u=2, e=2),
                    op=ADD,
                )

        def second_add(eng, g, k, lo, cnt):
            s0 = stream(k // NCH, (k % NCH) * JC)
            for off, n in pieces([s0 + lo, s0 + lo - 1], cnt):
                r = (s0 + lo + off) % NS
                rm = (s0 + lo + off - 1) % NS
                eng.tensor_tensor(
                    out=g[:, (lo + off) % 4 : (lo + off) % 4 + n, :],
                    in0=dv[:, r : r + n, 4:516],
                    in1=dv[:, rm : rm + n, 8:520],
                    op=ADD,
                )

        def emit_low_half(k, cnt):
            gg = ggpool.tile([P, 4, F_IN], BF16, align_bytes=64)
            gg_of[k] = gg
            if k == 0:
                nc.vector.memset(gg[:, 0, 0:16], 0.0)
            second_add(nc.gpsimd, gg, k, 0, cnt)

        def emit_plain(c):
            xc = xin_of[last][:].rearrange("p (j f t) -> p j t f", j=JC, t=4)
            po = pso.tile([P, 4, F_OUT], F32)
            j = 4 + c
            taps = [(j, adj), (j - 1, identb)] + ([(j + 1, identb)] if j + 1 < JC else [])
            for t in range(4):
                for n, (jj, moving) in enumerate(taps):
                    nc.tensor.matmul(
                        out=po[:, t, :], lhsT=xc[:, jj, t, :], rhs=moving[:], start=n == 0, stop=n == len(taps) - 1
                    )
            nc.scalar.copy(
                out=gp[:, c, :].rearrange("p (i t) -> p i t", t=4), in_=po[:].rearrange("p t i -> p i t")
            )

        def emit_high_half(k):
            gv = gvpool.tile([P, 4, F_IN], BF16, align_bytes=64)
            gv_of[k] = gv
            second_add(nc.vector, gv, k, 4, 4)

        def emit_quant(k, h, g, lo=0, hi=4):
            if k not in q_of:
                codes = qpool.tile([P, JC * P], U32, align_bytes=64)
                scl = qpool.tile([P, JC * P], U8, align_bytes=64)
                q_of[k] = (codes, scl)
            codes, scl = q_of[k]
            cols = slice((h * 4 + lo) * P, (h * 4 + hi) * P)
            nc.vector.quantize_mx(
                out=codes[:, cols].bitcast(FP8X4), scales=scl[:, cols], in_=g[:, lo:hi, :].rearrange("p j c -> p (j c)")
            )

        def emit_product(k, h):
            codes, scl = q_of[k]
            cols = slice(h * 4 * P, (h + 1) * 4 * P)
            py = psy.tile([P, 4 * P], F32)
            nc.tensor.matmul_mx(
                out=py[:],
                lhsT=wc[:].bitcast(FP8X4),
                lhsT_scale=ws[:],
                rhs=codes[:, cols].bitcast(FP8X4),
                rhs_scale=scl[:, cols],
                start=True,
                stop=True,
            )
            ysb = ypool.tile([P, 4 * P], F32)
            nc.scalar.activation(
                out=ysb[:], in_=py[:], func=mybir.ActivationFunctionType.Identity, bias=bcol[:, 0:1], scale=1.0
            )
            y_of[(k, h)] = ysb

        def out_tile(k):
            if k not in o_of:
                osb = opool.tile([P, JC, F_OUT], F32)
                o_of[k] = osb
            return o_of[k]

        def emit_turn_back(k, h):
            ysb = y_of[(k, h)]
            po = pso.tile([P, 4, F_OUT], F32)
            for a in range(4):
                nc.tensor.transpose(out=po[:, a, :], in_=ysb[:, a * P : (a + 1) * P], identity=ident[:])
            nc.scalar.copy(out=out_tile(k)[:, h * 4 : (h + 1) * 4, :], in_=po[:])

        def emit_direct(k, lo, cnt):
            codes, scl = q_of[k]
            po = pso.tile([P, 4, F_OUT], F32)
            for a in range(cnt):
                jl = lo + a
                nc.tensor.matmul_mx(
                    out=po[:, a, :],
                    lhsT=codes[:, jl * P : (jl + 1) * P].bitcast(FP8X4),
                    lhsT_scale=scl[:, jl * P : (jl + 1) * P],
                    rhs=wc[:].bitcast(FP8X4),
                    rhs_scale=ws[:],
                    start=True,
                    stop=True,
                )
            nc.vector.tensor_tensor(
                out=out_tile(k)[:, lo : lo + cnt, :], in0=po[:, 0:cnt, :], in1=bias4[:, 0:cnt, :], op=ADD
            )

        def emit_store(k, lo, cnt):
            bb, c = k // NCH, k % NCH
            a = (c * JC + lo) * F_OUT
            nc.sync.dma_start(
                out=outv[bb, :, a : a + cnt * F_OUT],
                in_=out_tile(k)[:, lo : lo + cnt, :].rearrange("p j o -> p (j o)"),
            )

        for k in range(3):
            emit_load(k)
        emit_constants()
        for m in range(4):
            emit_front(m)
        emit_edges(0)
        for m in range(3):
            emit_fill(m)
        last = n_chunks - 1
        for k in range(last):
            emit_pairsums(4 * k)
            if k >= 2:
                emit_product(k - 2, 0)
                emit_product(k - 2, 1)
            emit_front(4 * (k + 1))
            emit_fill(4 * k + 3)
            emit_pairsums(4 * k + 1)
            if k >= 2:
                emit_turn_back(k - 2, 0)
                emit_turn_back(k - 2, 1)
                emit_store(k - 2, 0, JC)
            if k + 1 == last:
                for c in range(2):
                    emit_plain(c)
            emit_pairsums(4 * k + 2)
            emit_pairsums(4 * k + 3)
            if k >= 1:
                emit_quant(k - 1, 1, gv_of[k - 1])
            emit_high_half(k)
            if k + 1 < last:
                emit_edges(k + 1)
            if k >= 1:
                emit_quant(k - 1, 0, gg_of[k - 1])
            emit_low_half(k, 4 if k + 1 < last else 2)
            pairs = 4 if k + 1 < last else 3
            for pair in range(1, pairs):
                emit_front(4 * (k + 1) + pair)
            for pair in range(pairs - 1):
                emit_fill(4 * (k + 1) + pair)
            if k + 3 < n_chunks:
                emit_load(k + 3)

        for c in range(2, 4):
            emit_plain(c)

        emit_pairsums(4 * last)
        for h in range(2):
            emit_product(last - 2, h)
        emit_pairsums(4 * last + 1)
        for h in range(2):
            emit_turn_back(last - 2, h)
        emit_store(last - 2, 0, JC)
        emit_quant(last - 1, 1, gv_of[last - 1])
        second_add(nc.vector, gg_of[last - 1], last - 1, 2, 2)
        emit_quant(last, 1, gp)
        emit_quant(last - 1, 0, gg_of[last - 1])
        gv = gvpool.tile([P, 4, F_IN], BF16, align_bytes=64)
        for lo in (0, 2):
            second_add(nc.vector, gv, last, lo, 2)
        for lo in (0, 2):
            emit_quant(last, 0, gv, lo, lo + 2)
        emit_product(last - 1, 1)
        emit_product(last, 1)
        emit_turn_back(last - 1, 1)
        emit_store(last - 1, 4, 4)
        emit_turn_back(last, 1)
        emit_store(last, 4, 4)
        emit_direct(last - 1, 0, 4)
        emit_store(last - 1, 0, 4)
        for lo in (0, 2):
            emit_direct(last, lo, 2)
            emit_store(last, lo, 2)
